import numpy as np
import ml_dtypes


def mxq(x, axis, fmt="e4m3"):
    dtype, down = {"e4m3": (ml_dtypes.float8_e4m3fn, 7), "e5m2": (ml_dtypes.float8_e5m2, 14)}[fmt]
    v = np.moveaxis(np.asarray(x, np.float32).astype(ml_dtypes.bfloat16).astype(np.float64), axis, -1)
    blocks = v.reshape(v.shape[:-1] + (-1, 32))
    amax = np.abs(blocks).max(-1, keepdims=True)
    byte = np.maximum(np.where(amax > 0, np.frexp(amax)[1] - 1 + 127, 0) - down, 1)
    scale = np.exp2(byte - 127.0)
    codes = (blocks / scale).astype(np.float32).astype(dtype).astype(np.float64)
    return np.moveaxis((codes * scale).reshape(v.shape), -1, axis)


WIDE = False


def mx_kscale(k):
    if not WIDE:
        return np.ones(k)
    levels = np.array([10, -10, 5, -5, 0])
    a = np.random.permutation(np.resize(levels, k // 512 * 4)).reshape(k // 512, 4)
    idx = np.arange(k)
    return np.exp2(a[idx // 512, idx % 128 // 32])


BF16 = ml_dtypes.bfloat16


def bf(x):
    return np.asarray(x, np.float32).astype(BF16)


def f64(x):
    return np.asarray(x).astype(np.float64)


N, IN_F, J, K = 256, 2048, 128, 16


def setup_inputs():
    s = mx_kscale(IN_F)
    s = s / s.max()
    return {"tensor": bf(np.random.standard_normal((N, IN_F)) * s),
            "T": bf(np.random.standard_normal((IN_F, J, K)) * 4.0 / (K * np.sqrt(IN_F)) / s[:, None, None])}


def reference(tensor, T):
    x = f64(tensor).reshape(tensor.shape[0], -1)
    feats = (mxq(x, 1, "e4m3") @ mxq(f64(T).reshape(IN_F, J * K), 0, "e4m3")).reshape(N, J, K)
    diversity = np.stack([np.exp(-np.abs(feats[n][None, :, :] - feats).sum(axis=2)).sum(axis=0) for n in range(N)])
    return np.concatenate((x, diversity), axis=1)

@@ -1,0 +1,263 @@
+from contextlib import ExitStack
+
+import concourse.mybir as mybir
+from concourse.masks import make_identity
+
+F32 = mybir.dt.float32
+BF16 = mybir.dt.bfloat16
+U32 = mybir.dt.uint32
+U8 = mybir.dt.uint8
+FP8X4 = mybir.dt.float8_e4m3fn_x4
+ALU = mybir.AluOpType
+ACT = mybir.ActivationFunctionType
+AXIS = mybir.AxisListType
+
+P = 128
+ROWS = 256
+ROW_BLOCKS = ROWS // P
+IN_F = 2048
+J = 128
+K = 16
+COLS = J * K
+PACK = 4
+K_PASS = P * PACK
+PASSES = IN_F // K_PASS
+BANK = 512
+COL_BLOCKS = COLS // BANK
+J_PER_BLOCK = BANK // K
+K_PER_BANK = BANK // ROWS
+F_BANKS = K // K_PER_BANK
+ROWS_PER_STEP = 4
+
+FLOPS = 2 * ROWS * IN_F * COLS
+
+
+def tile_minibatchdiscriminator_kernel(tc, tensor, T, out):
+    nc = tc.nc
+    weights = T.rearrange("i j k -> i (j k)")
+
+    with ExitStack() as pools:
+        keep = pools.enter_context(tc.tile_pool(name="keep", bufs=1))
+        banks = pools.enter_context(tc.psum_pool(name="banks", bufs=1))
+
+        identity = keep.tile([P, P], F32)
+        make_identity(nc, identity[:])
+
+        x_rows = keep.tile([P, ROW_BLOCKS * IN_F], BF16)
+        nc.sync.dma_start(
+            out=x_rows[:].rearrange("p (b i) -> p b i", b=ROW_BLOCKS),
+            in_=tensor.rearrange("(b p) i -> p b i", p=P),
+        )
+
+        f_sbuf = keep.tile([P, K, ROWS], F32)
+        f_banks = []
+        k_sum = keep.tile([P, ROWS], F32)
+        chain_start = keep.tile([P, ROWS], F32)
+        from_later = keep.tile([P, ROWS], F32)
+        from_earlier = keep.tile([P, ROWS_PER_STEP, ROWS], F32)
+        diversity = keep.tile([P, ROWS], F32)
+        d_rows = keep.tile([P, ROW_BLOCKS, J], F32)
+
+        with tc.tile_pool(name="stage", bufs=1) as stage:
+            t_raw = []
+            for g in range(PASSES):
+                raw = stage.tile([P, PACK, COLS], BF16, name="t_raw%d" % g)
+                for u in range(2):
+                    first = K_PASS * g + 2 * P * u
+                    nc.sync.dma_start(
+                        out=raw[:, 2 * u : 2 * u + 2, :],
+                        in_=weights[first : first + 2 * P, :].rearrange("(p e) c -> p e c", e=2),
+                    )
+                t_raw.append(raw)
+
+            x_words = x_rows[:].bitcast(F32)
+            words_per_row = IN_F // 2
+            x_grouped = stage.tile([P, PASSES * ROWS * PACK], BF16, align_bytes=64)
+            x_grouped_words = x_grouped[:].bitcast(F32).rearrange(
+                "p (g n u) -> p g n u", g=PASSES, u=2
+            )
+            for g in range(PASSES):
+                x_t = banks.tile([P, 2, ROWS], F32, name="x_t%d" % g, tag="bank%d" % g)
+                for u in range(2):
+                    for b in range(ROW_BLOCKS):
+                        first = words_per_row * b + 2 * P * g + P * u
+                        nc.tensor.transpose(
+                            x_t[:, u, b * P : (b + 1) * P],
+                            x_words[:, first : first + P],
+                            identity[:],
+                        )
+                nc.vector.tensor_copy(
+                    out=x_grouped_words[:, g], in_=x_t[:].rearrange("p u n -> p n u")
+                )
+            x_codes = stage.tile([P, PASSES, ROWS], U32, align_bytes=64)
+            x_scales = stage.tile([P, PASSES, ROWS], U8, align_bytes=64)
+            nc.vector.quantize_mx(
+                out=x_codes[:].rearrange("p g n -> p (g n)").bitcast(FP8X4),
+                scales=x_scales[:].rearrange("p g n -> p (g n)"),
+                in_=x_grouped[:],
+            )
+
+            t_codes = stage.tile([P, PASSES, COLS], U32, align_bytes=64)
+            t_scales = stage.tile([P, PASSES, COLS], U8, align_bytes=64)
+            feats = [
+                [
+                    banks.tile(
+                        [P, BANK],
+                        F32,
+                        name="feats%d_%d" % (b, c),
+                        tag="bank%d" % (COL_BLOCKS * b + c),
+                    )
+                    for c in range(COL_BLOCKS)
+                ]
+                for b in range(ROW_BLOCKS)
+            ]
+
+            def regroup(g, c):
+                grouped = stage.tile(
+                    [P, BANK, PACK], BF16, name="t_grouped", bufs=4, align_bytes=64
+                )
+                copy = nc.vector.tensor_copy if c % 2 == 0 else nc.scalar.copy
+                copy(
+                    out=grouped[:].rearrange("p (c i) t -> p c t i", i=4),
+                    in_=t_raw[g][:, :, c * BANK : (c + 1) * BANK].rearrange(
+                        "p t (c i) -> p c t i", i=4
+                    ),
+                )
+                return grouped
+
+            def quantise_and_multiply(grouped, g, c):
+                cols = slice(c * BANK, (c + 1) * BANK)
+                nc.vector.quantize_mx(
+                    out=t_codes[:, g, cols].bitcast(FP8X4),
+                    scales=t_scales[:, g, cols],
+                    in_=grouped[:].rearrange("p c t -> p (c t)"),
+                )
+                for b in range(ROW_BLOCKS):
+                    rows = slice(b * P, (b + 1) * P)
+                    nc.tensor.matmul_mx(
+                        out=feats[b][c][:],
+                        lhsT=x_codes[:, g, rows].bitcast(FP8X4),
+                        lhsT_scale=x_scales[:, g, rows],
+                        rhs=t_codes[:, g, cols].bitcast(FP8X4),
+                        rhs_scale=t_scales[:, g, cols],
+                        start=(g == 0),
+                        stop=(g == PASSES - 1),
+                    )
+
+            pieces = [(g, c) for g in range(PASSES) for c in range(COL_BLOCKS)]
+            waiting = None
+            for g, c in pieces:
+                grouped = regroup(g, c)
+                if waiting is not None:
+                    quantise_and_multiply(*waiting)
+                waiting = (grouped, g, c)
+            quantise_and_multiply(*waiting)
+
+            f_rows = [stage.tile([P, K, J], F32, name="f_rows%d" % b) for b in range(ROW_BLOCKS)]
+            for b in range(ROW_BLOCKS):
+                for c in range(COL_BLOCKS):
+                    copy = nc.vector.tensor_copy if c % 2 == 0 else nc.scalar.copy
+                    copy(
+                        out=f_rows[b][:, :, c * J_PER_BLOCK : (c + 1) * J_PER_BLOCK],
+                        in_=feats[b][c][:].rearrange("p (j k) -> p k j", k=K),
+                    )
+            for q in range(F_BANKS):
+                f_bank = banks.tile([P, K_PER_BANK, ROWS], F32, name="f_bank%d" % q, tag="bank%d" % q)
+                for h in range(K_PER_BANK):
+                    for b in range(ROW_BLOCKS):
+                        nc.tensor.transpose(
+                            f_bank[:, h, b * P : (b + 1) * P],
+                            f_rows[b][:, K_PER_BANK * q + h, :],
+                            identity[:],
+                        )
+                copy = nc.vector.tensor_copy if q % 2 == 0 else nc.scalar.copy
+                copy(out=f_sbuf[:, K_PER_BANK * q : K_PER_BANK * (q + 1), :], in_=f_bank[:])
+                f_banks.append(f_bank)
+
+        work = pools.enter_context(tc.tile_pool(name="work", bufs=3))
+
+        nc.vector.tensor_reduce(
+            out=k_sum[:], in_=f_sbuf[:].rearrange("p k n -> p n k"), axis=AXIS.X, op=ALU.add
+        )
+        nc.vector.tensor_scalar_mul(out=chain_start[:], in0=k_sum[:], scalar1=-0.5)
+
+        nc.vector.memset(from_later[:], 0.0)
+        nc.vector.memset(from_earlier[:], 0.0)
+
+        x_f32 = work.tile([P, ROW_BLOCKS * IN_F], F32, name="x_f32", bufs=1)
+        nc.scalar.copy(out=x_f32[:], in_=x_rows[:])
+        nc.sync.dma_start(
+            out=out[:, 0:IN_F].rearrange("(b p) i -> p b i", p=P),
+            in_=x_f32[:].rearrange("p (b i) -> p b i", b=ROW_BLOCKS),
+        )
+
+        steps = [
+            list(range(first, min(first + ROWS_PER_STEP, ROWS - 1)))
+            for first in range(0, ROWS - 1, ROWS_PER_STEP)
+        ]
+
+        def chains(rows):
+            acc = work.tile([P, ROWS_PER_STEP, ROWS], F32, name="acc")
+            for k in range(K):
+                for slot, n in enumerate(rows):
+                    later = slice(n + 1, ROWS)
+                    nc.vector.scalar_tensor_tensor(
+                        out=acc[:, slot, later],
+                        in0=f_banks[k // K_PER_BANK][:, k % K_PER_BANK, later],
+                        scalar=f_sbuf[:, k, n : n + 1],
+                        in1=chain_start[:, later] if k == 0 else acc[:, slot, later],
+                        op0=ALU.max,
+                        op1=ALU.add,
+                    )
+            return acc
+
+        def exponentials(rows, acc):
+            e = work.tile([P, ROWS_PER_STEP, ROWS], F32, name="e")
+            for slot, n in enumerate(rows):
+                later = slice(n + 1, ROWS)
+                nc.scalar.activation(
+                    out=e[:, slot, later],
+                    in_=acc[:, slot, later],
+                    func=ACT.Exp,
+                    bias=k_sum[:, n : n + 1],
+                    scale=-2.0,
+                    accum_out=from_later[:, n : n + 1],
+                )
+            return e
+
+        def add_to_later_rows(rows, e):
+            for slot, n in enumerate(rows):
+                later = slice(n + 1, ROWS)
+                nc.vector.tensor_tensor(
+                    out=from_earlier[:, slot, later],
+                    in0=from_earlier[:, slot, later],
+                    in1=e[:, slot, later],
+                    op=ALU.add,
+                )
+
+        pending = None
+        for rows in steps:
+            acc = chains(rows)
+            if pending is not None:
+                add_to_later_rows(*pending)
+            pending = (rows, exponentials(rows, acc))
+        add_to_later_rows(*pending)
+
+        nc.vector.tensor_reduce(
+            out=diversity[:], in_=from_earlier[:].rearrange("p s n -> p n s"), axis=AXIS.X, op=ALU.add
+        )
+        nc.vector.scalar_tensor_tensor(
+            out=diversity[:],
+            in0=diversity[:],
+            scalar=1.0,
+            in1=from_later[:],
+            op0=ALU.add,
+            op1=ALU.add,
+        )
+        d_t = banks.tile([P, ROW_BLOCKS, J], F32, name="d_t", tag="bank0")
+        for b in range(ROW_BLOCKS):
+            nc.tensor.transpose(d_t[:, b, :], diversity[:, b * P : (b + 1) * P], identity[:])
+        nc.vector.tensor_copy(out=d_rows[:], in_=d_t[:])
+        nc.sync.dma_start(
+            out=out[:, IN_F : IN_F + J].rearrange("(b p) j -> p b j", p=P), in_=d_rows[:]
+        )

@@ -27,7 +27,9 @@ COL_BLOCKS = COLS // BANK
 J_PER_BLOCK = BANK // K
 K_PER_BANK = BANK // ROWS
 F_BANKS = K // K_PER_BANK
-ROWS_PER_STEP = 4
+ROWS_PER_STEP = 6
+TREE_ROWS_PER_STEP = ROWS_PER_STEP // 3
+TREE_HALVES = (8, 4, 2, 1)
 
 FLOPS = 2 * ROWS * IN_F * COLS
 
@@ -180,9 +182,94 @@ def tile_minibatchdiscriminator_kernel(tc, tensor, T, out):
             out=k_sum[:], in_=f_sbuf[:].rearrange("p k n -> p n k"), axis=AXIS.X, op=ALU.add
         )
         nc.vector.tensor_scalar_mul(out=chain_start[:], in0=k_sum[:], scalar1=-0.5)
-
         nc.vector.memset(from_later[:], 0.0)
         nc.vector.memset(from_earlier[:], 0.0)
+
+        steps = [
+            list(range(first, min(first + ROWS_PER_STEP, ROWS - 1)))
+            for first in range(0, ROWS - 1, ROWS_PER_STEP)
+        ]
+
+        def chain_rows(rows):
+            return [n for n in rows if n % 3 != 2]
+
+        def tree_rows(rows):
+            return [n for n in rows if n % 3 == 2]
+
+        def chains(rows):
+            acc = work.tile([P, ROWS_PER_STEP, ROWS], F32, name="acc")
+            for k in range(K):
+                for n in rows:
+                    later = slice(n + 1, ROWS)
+                    nc.vector.scalar_tensor_tensor(
+                        out=acc[:, n % ROWS_PER_STEP, later],
+                        in0=f_banks[k // K_PER_BANK][:, k % K_PER_BANK, later],
+                        scalar=f_sbuf[:, k, n : n + 1],
+                        in1=chain_start[:, later] if k == 0 else acc[:, n % ROWS_PER_STEP, later],
+                        op0=ALU.max,
+                        op1=ALU.add,
+                    )
+            return acc
+
+        def absolute_differences(rows):
+            leaves = work.tile([P, TREE_ROWS_PER_STEP, K, ROWS], F32, name="leaves", bufs=2)
+            later = slice(rows[0] + 1, ROWS)
+            for r, n in enumerate(rows):
+                for k in range(K):
+                    nc.scalar.activation(
+                        out=leaves[:, r, k, later],
+                        in_=f_sbuf[:, k, later],
+                        func=ACT.Abs,
+                        bias=f_sbuf[:, k, n : n + 1],
+                        scale=-1.0,
+                    )
+            return leaves
+
+        def add_tree(rows, leaves):
+            later = slice(rows[0] + 1, ROWS)
+            for half in TREE_HALVES:
+                nc.gpsimd.tensor_tensor(
+                    out=leaves[:, 0 : len(rows), 0:half, later],
+                    in0=leaves[:, 0 : len(rows), 0:half, later],
+                    in1=leaves[:, 0 : len(rows), half : 2 * half, later],
+                    op=ALU.add,
+                )
+
+        def exponentials(rows, acc, leaves):
+            e = work.tile([P, ROWS_PER_STEP, ROWS], F32, name="e")
+            for n in chain_rows(rows):
+                later = slice(n + 1, ROWS)
+                nc.scalar.activation(
+                    out=e[:, n % ROWS_PER_STEP, later],
+                    in_=acc[:, n % ROWS_PER_STEP, later],
+                    func=ACT.Exp,
+                    bias=k_sum[:, n : n + 1],
+                    scale=-2.0,
+                    accum_out=from_later[:, n : n + 1],
+                )
+            for r, n in enumerate(tree_rows(rows)):
+                later = slice(n + 1, ROWS)
+                nc.scalar.activation(
+                    out=e[:, n % ROWS_PER_STEP, later],
+                    in_=leaves[:, r, 0, later],
+                    func=ACT.Exp,
+                    scale=-1.0,
+                    accum_out=from_later[:, n : n + 1],
+                )
+            return e
+
+        def add_to_later_rows(rows, e):
+            for n in rows:
+                later = slice(n + 1, ROWS)
+                engine = nc.gpsimd if n in tree_rows(rows) else nc.vector
+                engine.tensor_tensor(
+                    out=from_earlier[:, n % ROWS_PER_STEP, later],
+                    in0=from_earlier[:, n % ROWS_PER_STEP, later],
+                    in1=e[:, n % ROWS_PER_STEP, later],
+                    op=ALU.add,
+                )
+
+        leaves_ahead = absolute_differences(tree_rows(steps[0]))
 
         x_f32 = work.tile([P, ROW_BLOCKS * IN_F], F32, name="x_f32", bufs=1)
         nc.scalar.copy(out=x_f32[:], in_=x_rows[:])
@@ -191,56 +278,16 @@ def tile_minibatchdiscriminator_kernel(tc, tensor, T, out):
             in_=x_f32[:].rearrange("p (b i) -> p b i", b=ROW_BLOCKS),
         )
 
-        steps = [
-            list(range(first, min(first + ROWS_PER_STEP, ROWS - 1)))
-            for first in range(0, ROWS - 1, ROWS_PER_STEP)
-        ]
-
-        def chains(rows):
-            acc = work.tile([P, ROWS_PER_STEP, ROWS], F32, name="acc")
-            for k in range(K):
-                for slot, n in enumerate(rows):
-                    later = slice(n + 1, ROWS)
-                    nc.vector.scalar_tensor_tensor(
-                        out=acc[:, slot, later],
-                        in0=f_banks[k // K_PER_BANK][:, k % K_PER_BANK, later],
-                        scalar=f_sbuf[:, k, n : n + 1],
-                        in1=chain_start[:, later] if k == 0 else acc[:, slot, later],
-                        op0=ALU.max,
-                        op1=ALU.add,
-                    )
-            return acc
-
-        def exponentials(rows, acc):
-            e = work.tile([P, ROWS_PER_STEP, ROWS], F32, name="e")
-            for slot, n in enumerate(rows):
-                later = slice(n + 1, ROWS)
-                nc.scalar.activation(
-                    out=e[:, slot, later],
-                    in_=acc[:, slot, later],
-                    func=ACT.Exp,
-                    bias=k_sum[:, n : n + 1],
-                    scale=-2.0,
-                    accum_out=from_later[:, n : n + 1],
-                )
-            return e
-
-        def add_to_later_rows(rows, e):
-            for slot, n in enumerate(rows):
-                later = slice(n + 1, ROWS)
-                nc.vector.tensor_tensor(
-                    out=from_earlier[:, slot, later],
-                    in0=from_earlier[:, slot, later],
-                    in1=e[:, slot, later],
-                    op=ALU.add,
-                )
-
         pending = None
-        for rows in steps:
-            acc = chains(rows)
+        for index, rows in enumerate(steps):
+            leaves = leaves_ahead
+            if index + 1 < len(steps):
+                leaves_ahead = absolute_differences(tree_rows(steps[index + 1]))
+            acc = chains(chain_rows(rows))
+            add_tree(tree_rows(rows), leaves)
             if pending is not None:
                 add_to_later_rows(*pending)
-            pending = (rows, exponentials(rows, acc))
+            pending = (rows, exponentials(rows, acc, leaves))
         add_to_later_rows(*pending)
 
         nc.vector.tensor_reduce(

@@ -27,8 +27,9 @@ COL_BLOCKS = COLS // BANK
 J_PER_BLOCK = BANK // K
 K_PER_BANK = BANK // ROWS
 F_BANKS = K // K_PER_BANK
-ROWS_PER_STEP = 6
-TREE_ROWS_PER_STEP = ROWS_PER_STEP // 3
+VECTOR_ROWS = 100
+ROWS_PER_STEP = 4
+BATCH_PAIRS = 576
 TREE_HALVES = (8, 4, 2, 1)
 
 FLOPS = 2 * ROWS * IN_F * COLS
@@ -186,15 +187,15 @@ def tile_minibatchdiscriminator_kernel(tc, tensor, T, out):
         nc.vector.memset(from_earlier[:], 0.0)
 
         steps = [
-            list(range(first, min(first + ROWS_PER_STEP, ROWS - 1)))
-            for first in range(0, ROWS - 1, ROWS_PER_STEP)
+            list(range(first, first + ROWS_PER_STEP))
+            for first in range(0, VECTOR_ROWS, ROWS_PER_STEP)
         ]
-
-        def chain_rows(rows):
-            return [n for n in rows if n % 3 != 2]
-
-        def tree_rows(rows):
-            return [n for n in rows if n % 3 == 2]
+        batches = []
+        for n in range(VECTOR_ROWS, ROWS - 1):
+            if batches and (len(batches[-1]) + 1) * (ROWS - 1 - batches[-1][0]) <= BATCH_PAIRS:
+                batches[-1].append(n)
+            else:
+                batches.append([n])
 
         def chains(rows):
             acc = work.tile([P, ROWS_PER_STEP, ROWS], F32, name="acc")
@@ -211,33 +212,9 @@ def tile_minibatchdiscriminator_kernel(tc, tensor, T, out):
                     )
             return acc
 
-        def absolute_differences(rows):
-            leaves = work.tile([P, TREE_ROWS_PER_STEP, K, ROWS], F32, name="leaves", bufs=2)
-            later = slice(rows[0] + 1, ROWS)
-            for r, n in enumerate(rows):
-                for k in range(K):
-                    nc.scalar.activation(
-                        out=leaves[:, r, k, later],
-                        in_=f_sbuf[:, k, later],
-                        func=ACT.Abs,
-                        bias=f_sbuf[:, k, n : n + 1],
-                        scale=-1.0,
-                    )
-            return leaves
-
-        def add_tree(rows, leaves):
-            later = slice(rows[0] + 1, ROWS)
-            for half in TREE_HALVES:
-                nc.gpsimd.tensor_tensor(
-                    out=leaves[:, 0 : len(rows), 0:half, later],
-                    in0=leaves[:, 0 : len(rows), 0:half, later],
-                    in1=leaves[:, 0 : len(rows), half : 2 * half, later],
-                    op=ALU.add,
-                )
-
-        def exponentials(rows, acc, leaves):
-            e = work.tile([P, ROWS_PER_STEP, ROWS], F32, name="e")
-            for n in chain_rows(rows):
+        def chain_exponentials(rows, acc):
+            e = work.tile([P, ROWS_PER_STEP, ROWS], F32, name="e_step")
+            for n in rows:
                 later = slice(n + 1, ROWS)
                 nc.scalar.activation(
                     out=e[:, n % ROWS_PER_STEP, later],
@@ -247,29 +224,59 @@ def tile_minibatchdiscriminator_kernel(tc, tensor, T, out):
                     scale=-2.0,
                     accum_out=from_later[:, n : n + 1],
                 )
-            for r, n in enumerate(tree_rows(rows)):
-                later = slice(n + 1, ROWS)
+            return [(n, e[:, n % ROWS_PER_STEP, n + 1 : ROWS]) for n in rows]
+
+        def absolute_differences(rows):
+            width = ROWS - 1 - rows[0]
+            leaves = work.tile([P, K * BATCH_PAIRS], F32, name="leaves")
+            by_k_and_row = leaves[:, 0 : K * len(rows) * width].rearrange(
+                "p (k r m) -> p k r m", k=K, r=len(rows)
+            )
+            for r, n in enumerate(rows):
+                for k in range(K):
+                    nc.scalar.activation(
+                        out=by_k_and_row[:, k, r, :],
+                        in_=f_sbuf[:, k, rows[0] + 1 : ROWS],
+                        func=ACT.Abs,
+                        bias=f_sbuf[:, k, n : n + 1],
+                        scale=-1.0,
+                    )
+            return leaves
+
+        def add_tree(rows, leaves):
+            pairs = len(rows) * (ROWS - 1 - rows[0])
+            for half in TREE_HALVES:
+                nc.gpsimd.tensor_tensor(
+                    out=leaves[:, 0 : half * pairs],
+                    in0=leaves[:, 0 : half * pairs],
+                    in1=leaves[:, half * pairs : 2 * half * pairs],
+                    op=ALU.add,
+                )
+
+        def batch_exponentials(rows, leaves):
+            width = ROWS - 1 - rows[0]
+            e = work.tile([P, BATCH_PAIRS], F32, name="e_batch")
+            for r, n in enumerate(rows):
+                own = slice(r * width + r, (r + 1) * width)
                 nc.scalar.activation(
-                    out=e[:, n % ROWS_PER_STEP, later],
-                    in_=leaves[:, r, 0, later],
+                    out=e[:, own],
+                    in_=leaves[:, own],
                     func=ACT.Exp,
                     scale=-1.0,
                     accum_out=from_later[:, n : n + 1],
                 )
-            return e
+            return [(n, e[:, r * width + r : (r + 1) * width]) for r, n in enumerate(rows)]
 
-        def add_to_later_rows(rows, e):
-            for n in rows:
-                later = slice(n + 1, ROWS)
-                engine = nc.gpsimd if n in tree_rows(rows) else nc.vector
-                engine.tensor_tensor(
-                    out=from_earlier[:, n % ROWS_PER_STEP, later],
-                    in0=from_earlier[:, n % ROWS_PER_STEP, later],
-                    in1=e[:, n % ROWS_PER_STEP, later],
+        def add_to_later_rows(exponentials):
+            for n, e_row in exponentials:
+                nc.vector.tensor_tensor(
+                    out=from_earlier[:, n % ROWS_PER_STEP, n + 1 : ROWS],
+                    in0=from_earlier[:, n % ROWS_PER_STEP, n + 1 : ROWS],
+                    in1=e_row,
                     op=ALU.add,
                 )
 
-        leaves_ahead = absolute_differences(tree_rows(steps[0]))
+        leaves_ahead = absolute_differences(batches[0])
 
         x_f32 = work.tile([P, ROW_BLOCKS * IN_F], F32, name="x_f32", bufs=1)
         nc.scalar.copy(out=x_f32[:], in_=x_rows[:])
@@ -278,17 +285,22 @@ def tile_minibatchdiscriminator_kernel(tc, tensor, T, out):
             in_=x_f32[:].rearrange("p (b i) -> p b i", b=ROW_BLOCKS),
         )
 
-        pending = None
-        for index, rows in enumerate(steps):
+        exponentials = []
+        for t in range(max(len(steps), len(batches))):
             leaves = leaves_ahead
-            if index + 1 < len(steps):
-                leaves_ahead = absolute_differences(tree_rows(steps[index + 1]))
-            acc = chains(chain_rows(rows))
-            add_tree(tree_rows(rows), leaves)
-            if pending is not None:
-                add_to_later_rows(*pending)
-            pending = (rows, exponentials(rows, acc, leaves))
-        add_to_later_rows(*pending)
+            if t + 1 < len(batches):
+                leaves_ahead = absolute_differences(batches[t + 1])
+            if t < len(steps):
+                acc = chains(steps[t])
+            if t < len(batches):
+                add_tree(batches[t], leaves)
+            add_to_later_rows(exponentials)
+            exponentials = []
+            if t < len(steps):
+                exponentials.extend(chain_exponentials(steps[t], acc))
+            if t < len(batches):
+                exponentials.extend(batch_exponentials(batches[t], leaves))
+        add_to_later_rows(exponentials)
 
         nc.vector.tensor_reduce(
             out=diversity[:], in_=from_earlier[:].rearrange("p s n -> p n s"), axis=AXIS.X, op=ALU.add

@@ -27,9 +27,8 @@ COL_BLOCKS = COLS // BANK
 J_PER_BLOCK = BANK // K
 K_PER_BANK = BANK // ROWS
 F_BANKS = K // K_PER_BANK
-VECTOR_ROWS = 100
-ROWS_PER_STEP = 4
-BATCH_PAIRS = 576
+ROWS_PER_STEP = 9
+TREE_ROWS = 3
 TREE_HALVES = (8, 4, 2, 1)
 
 FLOPS = 2 * ROWS * IN_F * COLS
@@ -57,7 +56,7 @@ def tile_minibatchdiscriminator_kernel(tc, tensor, T, out):
         k_sum = keep.tile([P, ROWS], F32)
         chain_start = keep.tile([P, ROWS], F32)
         from_later = keep.tile([P, ROWS], F32)
-        from_earlier = keep.tile([P, ROWS_PER_STEP, ROWS], F32)
+        from_earlier = keep.tile([P, ROWS], F32)
         diversity = keep.tile([P, ROWS], F32)
         d_rows = keep.tile([P, ROW_BLOCKS, J], F32)
 
@@ -187,48 +186,19 @@ def tile_minibatchdiscriminator_kernel(tc, tensor, T, out):
         nc.vector.memset(from_earlier[:], 0.0)
 
         steps = [
-            list(range(first, first + ROWS_PER_STEP))
-            for first in range(0, VECTOR_ROWS, ROWS_PER_STEP)
+            list(range(first, min(first + ROWS_PER_STEP, ROWS - 1)))
+            for first in range(0, ROWS - 1, ROWS_PER_STEP)
         ]
-        batches = []
-        for n in range(VECTOR_ROWS, ROWS - 1):
-            if batches and (len(batches[-1]) + 1) * (ROWS - 1 - batches[-1][0]) <= BATCH_PAIRS:
-                batches[-1].append(n)
-            else:
-                batches.append([n])
 
-        def chains(rows):
-            acc = work.tile([P, ROWS_PER_STEP, ROWS], F32, name="acc")
-            for k in range(K):
-                for n in rows:
-                    later = slice(n + 1, ROWS)
-                    nc.vector.scalar_tensor_tensor(
-                        out=acc[:, n % ROWS_PER_STEP, later],
-                        in0=f_banks[k // K_PER_BANK][:, k % K_PER_BANK, later],
-                        scalar=f_sbuf[:, k, n : n + 1],
-                        in1=chain_start[:, later] if k == 0 else acc[:, n % ROWS_PER_STEP, later],
-                        op0=ALU.max,
-                        op1=ALU.add,
-                    )
-            return acc
+        def tree_rows(t):
+            return steps[t][:TREE_ROWS] if 0 <= t < len(steps) else []
 
-        def chain_exponentials(rows, acc):
-            e = work.tile([P, ROWS_PER_STEP, ROWS], F32, name="e_step")
-            for n in rows:
-                later = slice(n + 1, ROWS)
-                nc.scalar.activation(
-                    out=e[:, n % ROWS_PER_STEP, later],
-                    in_=acc[:, n % ROWS_PER_STEP, later],
-                    func=ACT.Exp,
-                    bias=k_sum[:, n : n + 1],
-                    scale=-2.0,
-                    accum_out=from_later[:, n : n + 1],
-                )
-            return [(n, e[:, n % ROWS_PER_STEP, n + 1 : ROWS]) for n in rows]
+        def chain_rows(t):
+            return steps[t][TREE_ROWS:] if 0 <= t < len(steps) else []
 
         def absolute_differences(rows):
             width = ROWS - 1 - rows[0]
-            leaves = work.tile([P, K * BATCH_PAIRS], F32, name="leaves")
+            leaves = work.tile([P, K * TREE_ROWS * (ROWS - 1)], F32, name="leaves")
             by_k_and_row = leaves[:, 0 : K * len(rows) * width].rearrange(
                 "p (k r m) -> p k r m", k=K, r=len(rows)
             )
@@ -253,61 +223,102 @@ def tile_minibatchdiscriminator_kernel(tc, tensor, T, out):
                     op=ALU.add,
                 )
 
-        def batch_exponentials(rows, leaves):
-            width = ROWS - 1 - rows[0]
-            e = work.tile([P, BATCH_PAIRS], F32, name="e_batch")
-            for r, n in enumerate(rows):
-                own = slice(r * width + r, (r + 1) * width)
+        def chains(rows):
+            acc = work.tile([P, ROWS_PER_STEP - TREE_ROWS, ROWS], F32, name="acc")
+            for k in range(K):
+                for c, n in enumerate(rows):
+                    later = slice(n + 1, ROWS)
+                    nc.vector.scalar_tensor_tensor(
+                        out=acc[:, c, later],
+                        in0=f_banks[k // K_PER_BANK][:, k % K_PER_BANK, later],
+                        scalar=f_sbuf[:, k, n : n + 1],
+                        in1=chain_start[:, later] if k == 0 else acc[:, c, later],
+                        op0=ALU.max,
+                        op1=ALU.add,
+                    )
+            return acc
+
+        def zeroed_corner(rows):
+            e = work.tile([P, ROWS_PER_STEP, ROWS], F32, name="e")
+            nc.vector.memset(e[:, 0 : len(rows), rows[0] + 1 : rows[-1] + 2], 0.0)
+            return e
+
+        def exponentials(e, from_tree, leaves, from_chains, acc):
+            for r, n in enumerate(from_tree):
+                width = ROWS - 1 - from_tree[0]
                 nc.scalar.activation(
-                    out=e[:, own],
-                    in_=leaves[:, own],
+                    out=e[:, r, n + 1 : ROWS],
+                    in_=leaves[:, r * width + r : (r + 1) * width],
                     func=ACT.Exp,
                     scale=-1.0,
                     accum_out=from_later[:, n : n + 1],
                 )
-            return [(n, e[:, r * width + r : (r + 1) * width]) for r, n in enumerate(rows)]
-
-        def add_to_later_rows(exponentials):
-            for n, e_row in exponentials:
-                nc.vector.tensor_tensor(
-                    out=from_earlier[:, n % ROWS_PER_STEP, n + 1 : ROWS],
-                    in0=from_earlier[:, n % ROWS_PER_STEP, n + 1 : ROWS],
-                    in1=e_row,
-                    op=ALU.add,
+            for c, n in enumerate(from_chains):
+                nc.scalar.activation(
+                    out=e[:, len(from_tree) + c, n + 1 : ROWS],
+                    in_=acc[:, c, n + 1 : ROWS],
+                    func=ACT.Exp,
+                    bias=k_sum[:, n : n + 1],
+                    scale=-2.0,
+                    accum_out=from_later[:, n : n + 1],
                 )
 
-        leaves_ahead = absolute_differences(batches[0])
+        def sum_over_rows(rows, e):
+            later = slice(rows[0] + 1, ROWS)
+            row_sum = work.tile([P, ROWS], F32, name="row_sum")
+            nc.vector.tensor_reduce(
+                out=row_sum[:, later],
+                in_=e[:, 0 : len(rows), later].rearrange("p r m -> p m r"),
+                axis=AXIS.X,
+                op=ALU.add,
+            )
+            return (later, row_sum)
 
-        x_f32 = work.tile([P, ROW_BLOCKS * IN_F], F32, name="x_f32", bufs=1)
-        nc.scalar.copy(out=x_f32[:], in_=x_rows[:])
-        nc.sync.dma_start(
-            out=out[:, 0:IN_F].rearrange("(b p) i -> p b i", p=P),
-            in_=x_f32[:].rearrange("p (b i) -> p b i", b=ROW_BLOCKS),
-        )
+        def add_to_later_rows(later, row_sum):
+            nc.gpsimd.tensor_tensor(
+                out=from_earlier[:, later],
+                in0=from_earlier[:, later],
+                in1=row_sum[:, later],
+                op=ALU.add,
+            )
 
-        exponentials = []
-        for t in range(max(len(steps), len(batches))):
-            leaves = leaves_ahead
-            if t + 1 < len(batches):
-                leaves_ahead = absolute_differences(batches[t + 1])
-            if t < len(steps):
-                acc = chains(steps[t])
-            if t < len(batches):
-                add_tree(batches[t], leaves)
-            add_to_later_rows(exponentials)
-            exponentials = []
-            if t < len(steps):
-                exponentials.extend(chain_exponentials(steps[t], acc))
-            if t < len(batches):
-                exponentials.extend(batch_exponentials(batches[t], leaves))
-        add_to_later_rows(exponentials)
+        leaves_of = {}
+        acc_of = {}
+        e_of = {}
+        unadded = None
+        with tc.manual_schedule():
+            leaves_of[0] = absolute_differences(tree_rows(0))
 
-        nc.vector.tensor_reduce(
-            out=diversity[:], in_=from_earlier[:].rearrange("p s n -> p n s"), axis=AXIS.X, op=ALU.add
-        )
+            for b in range(ROW_BLOCKS):
+                x_f32 = work.tile([P, IN_F], F32, name="x_f32", bufs=1)
+                nc.scalar.copy(out=x_f32[:], in_=x_rows[:, b * IN_F : (b + 1) * IN_F])
+                nc.sync.dma_start(out=out[b * P : (b + 1) * P, 0:IN_F], in_=x_f32[:])
+
+            for t in range(len(steps) + 2):
+                done = tree_rows(t - 2) + chain_rows(t - 1)
+                if done:
+                    exponentials(
+                        e_of[t], tree_rows(t - 2), leaves_of.get(t - 2), chain_rows(t - 1), acc_of.get(t - 1)
+                    )
+                if tree_rows(t + 1):
+                    leaves_of[t + 1] = absolute_differences(tree_rows(t + 1))
+                done_next = tree_rows(t - 1) + chain_rows(t)
+                if done_next:
+                    e_of[t + 1] = zeroed_corner(done_next)
+                if chain_rows(t):
+                    acc_of[t] = chains(chain_rows(t))
+                if tree_rows(t):
+                    add_tree(tree_rows(t), leaves_of[t])
+                if unadded is not None:
+                    add_to_later_rows(*unadded)
+                    unadded = None
+                if done:
+                    unadded = sum_over_rows(done, e_of[t])
+            add_to_later_rows(*unadded)
+
         nc.vector.scalar_tensor_tensor(
             out=diversity[:],
-            in0=diversity[:],
+            in0=from_earlier[:],
             scalar=1.0,
             in1=from_later[:],
             op0=ALU.add,

from contextlib import ExitStack

import concourse.mybir as mybir
from concourse.masks import make_identity

F32 = mybir.dt.float32
BF16 = mybir.dt.bfloat16
U32 = mybir.dt.uint32
U8 = mybir.dt.uint8
FP8X4 = mybir.dt.float8_e4m3fn_x4
ALU = mybir.AluOpType
ACT = mybir.ActivationFunctionType
AXIS = mybir.AxisListType

P = 128
ROWS = 256
ROW_BLOCKS = ROWS // P
IN_F = 2048
J = 128
K = 16
COLS = J * K
PACK = 4
K_PASS = P * PACK
PASSES = IN_F // K_PASS
BANK = 512
COL_BLOCKS = COLS // BANK
J_PER_BLOCK = BANK // K
K_PER_BANK = BANK // ROWS
F_BANKS = K // K_PER_BANK
ROWS_PER_STEP = 9
TREE_ROWS = 3
TREE_HALVES = (8, 4, 2, 1)

FLOPS = 2 * ROWS * IN_F * COLS


def tile_minibatchdiscriminator_kernel(tc, tensor, T, out):
    nc = tc.nc
    weights = T.rearrange("i j k -> i (j k)")

    with ExitStack() as pools:
        keep = pools.enter_context(tc.tile_pool(name="keep", bufs=1))
        banks = pools.enter_context(tc.psum_pool(name="banks", bufs=1))

        identity = keep.tile([P, P], F32)
        make_identity(nc, identity[:])

        x_rows = keep.tile([P, ROW_BLOCKS * IN_F], BF16)
        nc.sync.dma_start(
            out=x_rows[:].rearrange("p (b i) -> p b i", b=ROW_BLOCKS),
            in_=tensor.rearrange("(b p) i -> p b i", p=P),
        )

        f_sbuf = keep.tile([P, K, ROWS], F32)
        f_banks = []
        k_sum = keep.tile([P, ROWS], F32)
        chain_start = keep.tile([P, ROWS], F32)
        from_later = keep.tile([P, ROWS], F32)
        from_earlier = keep.tile([P, ROWS], F32)
        diversity = keep.tile([P, ROWS], F32)
        d_rows = keep.tile([P, ROW_BLOCKS, J], F32)

        with tc.tile_pool(name="stage", bufs=1) as stage:
            t_raw = []
            for g in range(PASSES):
                raw = stage.tile([P, PACK, COLS], BF16, name="t_raw%d" % g)
                for u in range(2):
                    first = K_PASS * g + 2 * P * u
                    nc.sync.dma_start(
                        out=raw[:, 2 * u : 2 * u + 2, :],
                        in_=weights[first : first + 2 * P, :].rearrange("(p e) c -> p e c", e=2),
                    )
                t_raw.append(raw)

            x_words = x_rows[:].bitcast(F32)
            words_per_row = IN_F // 2
            x_grouped = stage.tile([P, PASSES * ROWS * PACK], BF16, align_bytes=64)
            x_grouped_words = x_grouped[:].bitcast(F32).rearrange(
                "p (g n u) -> p g n u", g=PASSES, u=2
            )
            for g in range(PASSES):
                x_t = banks.tile([P, 2, ROWS], F32, name="x_t%d" % g, tag="bank%d" % g)
                for u in range(2):
                    for b in range(ROW_BLOCKS):
                        first = words_per_row * b + 2 * P * g + P * u
                        nc.tensor.transpose(
                            x_t[:, u, b * P : (b + 1) * P],
                            x_words[:, first : first + P],
                            identity[:],
                        )
                nc.vector.tensor_copy(
                    out=x_grouped_words[:, g], in_=x_t[:].rearrange("p u n -> p n u")
                )
            x_codes = stage.tile([P, PASSES, ROWS], U32, align_bytes=64)
            x_scales = stage.tile([P, PASSES, ROWS], U8, align_bytes=64)
            nc.vector.quantize_mx(
                out=x_codes[:].rearrange("p g n -> p (g n)").bitcast(FP8X4),
                scales=x_scales[:].rearrange("p g n -> p (g n)"),
                in_=x_grouped[:],
            )

            t_codes = stage.tile([P, PASSES, COLS], U32, align_bytes=64)
            t_scales = stage.tile([P, PASSES, COLS], U8, align_bytes=64)
            feats = [
                [
                    banks.tile(
                        [P, BANK],
                        F32,
                        name="feats%d_%d" % (b, c),
                        tag="bank%d" % (COL_BLOCKS * b + c),
                    )
                    for c in range(COL_BLOCKS)
                ]
                for b in range(ROW_BLOCKS)
            ]

            def regroup(g, c):
                grouped = stage.tile(
                    [P, BANK, PACK], BF16, name="t_grouped", bufs=4, align_bytes=64
                )
                copy = nc.vector.tensor_copy if c % 2 == 0 else nc.scalar.copy
                copy(
                    out=grouped[:].rearrange("p (c i) t -> p c t i", i=4),
                    in_=t_raw[g][:, :, c * BANK : (c + 1) * BANK].rearrange(
                        "p t (c i) -> p c t i", i=4
                    ),
                )
                return grouped

            def quantise_and_multiply(grouped, g, c):
                cols = slice(c * BANK, (c + 1) * BANK)
                nc.vector.quantize_mx(
                    out=t_codes[:, g, cols].bitcast(FP8X4),
                    scales=t_scales[:, g, cols],
                    in_=grouped[:].rearrange("p c t -> p (c t)"),
                )
                for b in range(ROW_BLOCKS):
                    rows = slice(b * P, (b + 1) * P)
                    nc.tensor.matmul_mx(
                        out=feats[b][c][:],
                        lhsT=x_codes[:, g, rows].bitcast(FP8X4),
                        lhsT_scale=x_scales[:, g, rows],
                        rhs=t_codes[:, g, cols].bitcast(FP8X4),
                        rhs_scale=t_scales[:, g, cols],
                        start=(g == 0),
                        stop=(g == PASSES - 1),
                    )

            pieces = [(g, c) for g in range(PASSES) for c in range(COL_BLOCKS)]
            waiting = None
            for g, c in pieces:
                grouped = regroup(g, c)
                if waiting is not None:
                    quantise_and_multiply(*waiting)
                waiting = (grouped, g, c)
            quantise_and_multiply(*waiting)

            f_rows = [stage.tile([P, K, J], F32, name="f_rows%d" % b) for b in range(ROW_BLOCKS)]
            for b in range(ROW_BLOCKS):
                for c in range(COL_BLOCKS):
                    copy = nc.vector.tensor_copy if c % 2 == 0 else nc.scalar.copy
                    copy(
                        out=f_rows[b][:, :, c * J_PER_BLOCK : (c + 1) * J_PER_BLOCK],
                        in_=feats[b][c][:].rearrange("p (j k) -> p k j", k=K),
                    )
            for q in range(F_BANKS):
                f_bank = banks.tile([P, K_PER_BANK, ROWS], F32, name="f_bank%d" % q, tag="bank%d" % q)
                for h in range(K_PER_BANK):
                    for b in range(ROW_BLOCKS):
                        nc.tensor.transpose(
                            f_bank[:, h, b * P : (b + 1) * P],
                            f_rows[b][:, K_PER_BANK * q + h, :],
                            identity[:],
                        )
                copy = nc.vector.tensor_copy if q % 2 == 0 else nc.scalar.copy
                copy(out=f_sbuf[:, K_PER_BANK * q : K_PER_BANK * (q + 1), :], in_=f_bank[:])
                f_banks.append(f_bank)

        work = pools.enter_context(tc.tile_pool(name="work", bufs=3))

        nc.vector.tensor_reduce(
            out=k_sum[:], in_=f_sbuf[:].rearrange("p k n -> p n k"), axis=AXIS.X, op=ALU.add
        )
        nc.vector.tensor_scalar_mul(out=chain_start[:], in0=k_sum[:], scalar1=-0.5)
        nc.vector.memset(from_later[:], 0.0)
        nc.vector.memset(from_earlier[:], 0.0)

        steps = [
            list(range(first, min(first + ROWS_PER_STEP, ROWS - 1)))
            for first in range(0, ROWS - 1, ROWS_PER_STEP)
        ]

        def tree_rows(t):
            return steps[t][:TREE_ROWS] if 0 <= t < len(steps) else []

        def chain_rows(t):
            return steps[t][TREE_ROWS:] if 0 <= t < len(steps) else []

        def absolute_differences(rows):
            width = ROWS - 1 - rows[0]
            leaves = work.tile([P, K * TREE_ROWS * (ROWS - 1)], F32, name="leaves")
            by_k_and_row = leaves[:, 0 : K * len(rows) * width].rearrange(
                "p (k r m) -> p k r m", k=K, r=len(rows)
            )
            for r, n in enumerate(rows):
                for k in range(K):
                    nc.scalar.activation(
                        out=by_k_and_row[:, k, r, :],
                        in_=f_sbuf[:, k, rows[0] + 1 : ROWS],
                        func=ACT.Abs,
                        bias=f_sbuf[:, k, n : n + 1],
                        scale=-1.0,
                    )
            return leaves

        def add_tree(rows, leaves):
            pairs = len(rows) * (ROWS - 1 - rows[0])
            for half in TREE_HALVES:
                nc.gpsimd.tensor_tensor(
                    out=leaves[:, 0 : half * pairs],
                    in0=leaves[:, 0 : half * pairs],
                    in1=leaves[:, half * pairs : 2 * half * pairs],
                    op=ALU.add,
                )

        def chains(rows):
            acc = work.tile([P, ROWS_PER_STEP - TREE_ROWS, ROWS], F32, name="acc")
            for k in range(K):
                for c, n in enumerate(rows):
                    later = slice(n + 1, ROWS)
                    nc.vector.scalar_tensor_tensor(
                        out=acc[:, c, later],
                        in0=f_banks[k // K_PER_BANK][:, k % K_PER_BANK, later],
                        scalar=f_sbuf[:, k, n : n + 1],
                        in1=chain_start[:, later] if k == 0 else acc[:, c, later],
                        op0=ALU.max,
                        op1=ALU.add,
                    )
            return acc

        def zeroed_corner(rows):
            e = work.tile([P, ROWS_PER_STEP, ROWS], F32, name="e")
            nc.vector.memset(e[:, 0 : len(rows), rows[0] + 1 : rows[-1] + 2], 0.0)
            return e

        def exponentials(e, from_tree, leaves, from_chains, acc):
            for r, n in enumerate(from_tree):
                width = ROWS - 1 - from_tree[0]
                nc.scalar.activation(
                    out=e[:, r, n + 1 : ROWS],
                    in_=leaves[:, r * width + r : (r + 1) * width],
                    func=ACT.Exp,
                    scale=-1.0,
                    accum_out=from_later[:, n : n + 1],
                )
            for c, n in enumerate(from_chains):
                nc.scalar.activation(
                    out=e[:, len(from_tree) + c, n + 1 : ROWS],
                    in_=acc[:, c, n + 1 : ROWS],
                    func=ACT.Exp,
                    bias=k_sum[:, n : n + 1],
                    scale=-2.0,
                    accum_out=from_later[:, n : n + 1],
                )

        def sum_over_rows(rows, e):
            later = slice(rows[0] + 1, ROWS)
            row_sum = work.tile([P, ROWS], F32, name="row_sum")
            nc.vector.tensor_reduce(
                out=row_sum[:, later],
                in_=e[:, 0 : len(rows), later].rearrange("p r m -> p m r"),
                axis=AXIS.X,
                op=ALU.add,
            )
            return (later, row_sum)

        def add_to_later_rows(later, row_sum):
            nc.gpsimd.tensor_tensor(
                out=from_earlier[:, later],
                in0=from_earlier[:, later],
                in1=row_sum[:, later],
                op=ALU.add,
            )

        leaves_of = {}
        acc_of = {}
        e_of = {}
        unadded = None
        with tc.manual_schedule():
            leaves_of[0] = absolute_differences(tree_rows(0))

            for b in range(ROW_BLOCKS):
                x_f32 = work.tile([P, IN_F], F32, name="x_f32", bufs=1)
                nc.scalar.copy(out=x_f32[:], in_=x_rows[:, b * IN_F : (b + 1) * IN_F])
                nc.sync.dma_start(out=out[b * P : (b + 1) * P, 0:IN_F], in_=x_f32[:])

            for t in range(len(steps) + 2):
                done = tree_rows(t - 2) + chain_rows(t - 1)
                if done:
                    exponentials(
                        e_of[t], tree_rows(t - 2), leaves_of.get(t - 2), chain_rows(t - 1), acc_of.get(t - 1)
                    )
                if tree_rows(t + 1):
                    leaves_of[t + 1] = absolute_differences(tree_rows(t + 1))
                done_next = tree_rows(t - 1) + chain_rows(t)
                if done_next:
                    e_of[t + 1] = zeroed_corner(done_next)
                if chain_rows(t):
                    acc_of[t] = chains(chain_rows(t))
                if tree_rows(t):
                    add_tree(tree_rows(t), leaves_of[t])
                if unadded is not None:
                    add_to_later_rows(*unadded)
                    unadded = None
                if done:
                    unadded = sum_over_rows(done, e_of[t])
            add_to_later_rows(*unadded)

        nc.vector.scalar_tensor_tensor(
            out=diversity[:],
            in0=from_earlier[:],
            scalar=1.0,
            in1=from_later[:],
            op0=ALU.add,
            op1=ALU.add,
        )
        d_t = banks.tile([P, ROW_BLOCKS, J], F32, name="d_t", tag="bank0")
        for b in range(ROW_BLOCKS):
            nc.tensor.transpose(d_t[:, b, :], diversity[:, b * P : (b + 1) * P], identity[:])
        nc.vector.tensor_copy(out=d_rows[:], in_=d_t[:])
        nc.sync.dma_start(
            out=out[:, IN_F : IN_F + J].rearrange("(b p) j -> p b j", p=P), in_=d_rows[:]
        )
